import numpy as np
import ml_dtypes


def mxq(x, axis, fmt="e4m3"):
    dtype, down = {"e4m3": (ml_dtypes.float8_e4m3fn, 7), "e5m2": (ml_dtypes.float8_e5m2, 14)}[fmt]
    v = np.moveaxis(np.asarray(x, np.float32).astype(ml_dtypes.bfloat16).astype(np.float64), axis, -1)
    blocks = v.reshape(v.shape[:-1] + (-1, 32))
    amax = np.abs(blocks).max(-1, keepdims=True)
    byte = np.maximum(np.where(amax > 0, np.frexp(amax)[1] - 1 + 127, 0) - down, 1)
    scale = np.exp2(byte - 127.0)
    codes = (blocks / scale).astype(np.float32).astype(dtype).astype(np.float64)
    return np.moveaxis((codes * scale).reshape(v.shape), -1, axis)


WIDE = False


def mx_kscale(k):
    if not WIDE:
        return np.ones(k)
    levels = np.array([10, -10, 5, -5, 0])
    a = np.random.permutation(np.resize(levels, k // 512 * 4)).reshape(k // 512, 4)
    idx = np.arange(k)
    return np.exp2(a[idx // 512, idx % 128 // 32])


BF16 = ml_dtypes.bfloat16


def bf(x):
    return np.asarray(x, np.float32).astype(BF16)


def f64(x):
    return np.asarray(x).astype(np.float64)


B, OBS, ACT, U, KSUB = 4096, 383, 128, 1024, 2
DT = 1.0 / KSUB
LN_EPS = 1e-5


def mish(v):
    return v * np.tanh(np.log(1.0 + np.exp(v)))


def layer_norm(v, g, b):
    mu = v.mean(-1, keepdims=True)
    var = np.square(v - mu).mean(-1, keepdims=True)
    return (v - mu) / np.sqrt(var + LN_EPS) * g + b


def setup_inputs():
    s, t = mx_kscale(U), mx_kscale(U)
    return {"h0": bf(np.random.standard_normal((B, U)) * s),
            "z": bf(np.random.standard_normal((B, ACT)) * 0.5),
            "k1": bf(np.random.standard_normal((B, ACT))),
            "W1": bf(np.random.standard_normal((U, U)) / np.sqrt(U) / s[:, None]),
            "b1": bf(np.random.standard_normal(U) * 0.3),
            "ln1_g": bf((1.0 + 0.1 * np.random.standard_normal(U)) * t),
            "ln1_b": bf(0.1 * np.random.standard_normal(U) * t),
            "W2": bf(np.random.standard_normal((U, ACT)) / np.sqrt(U) / t[:, None]),
            "b2": bf(np.random.standard_normal(ACT) * 0.3)}


def reference(h0, z, k1, W1, b1, ln1_g, ln1_b, W2, b2):
    h1 = layer_norm(mish((mxq(f64(h0), 1, "e4m3") @ mxq(f64(W1), 0, "e4m3")) + f64(b1)), f64(ln1_g), f64(ln1_b))
    k2 = (mxq(h1, 1, "e4m3") @ mxq(f64(W2), 0, "e4m3")) + f64(b2)
    return f64(z) + (DT / 2.0) * (f64(k1) + k2)

@@ -1,0 +1,325 @@
+from contextlib import ExitStack
+
+import concourse.mybir as mybir
+from concourse.masks import make_identity
+
+F32 = mybir.dt.float32
+BF16 = mybir.dt.bfloat16
+U32 = mybir.dt.uint32
+U8 = mybir.dt.uint8
+FP8X4 = mybir.dt.float8_e4m3fn_x4
+FUNC = mybir.ActivationFunctionType
+ALU = mybir.AluOpType
+
+P = 128
+BATCH, HID, OUT = 4096, 1024, 128
+TILES = BATCH // P
+QUAD = 4
+QUADS = TILES // QUAD
+PACK = 4
+K_PASS = P * PACK
+PASSES = HID // K_PASS
+BANK = 512
+HALVES = HID // BANK
+U_TILES = HID // P
+LN_EPS = 1e-5
+STEP = 0.25
+
+FLOPS = 2 * BATCH * HID * (HID + OUT)
+
+
+def interleave_four(copy, dst, src):
+    copy(
+        out=dst.rearrange("p (c i) t -> p c t i", i=4),
+        in_=src.rearrange("p t (c i) -> p c t i", i=4),
+    )
+
+
+def tile_actorflowode_pb_t_kernel(tc, h0, z, k1, W1, b1, ln1_g, ln1_b, W2, b2, out):
+    nc = tc.nc
+    h0_rows = h0.rearrange("(p n) k -> p n k", n=TILES)
+    z_rows = z.rearrange("(p n) c -> p n c", n=TILES)
+    k1_rows = k1.rearrange("(p n) c -> p n c", n=TILES)
+    out_rows = out.rearrange("(p n) c -> p n c", n=TILES)
+
+    with ExitStack() as ctx:
+        ctx.enter_context(tc.manual_schedule())
+        keep = ctx.enter_context(tc.tile_pool(name="keep", bufs=1))
+        feed = ctx.enter_context(tc.tile_pool(name="feed", bufs=1))
+        psum = ctx.enter_context(tc.psum_pool(name="psum", bufs=1))
+
+        h0_sb, h0_grouped, h0_codes, h0_scales = {}, {}, {}, {}
+        pre, act, stats, rstd = {}, {}, {}, {}
+        h1, h1_codes, h1_scales, head, base = {}, {}, {}, {}, {}
+
+        def load_h0(q):
+            h0_sb[q] = feed.tile([P, QUAD, HID], BF16, name="h0_sb", bufs=3)
+            nc.sync.dma_start(out=h0_sb[q][:], in_=h0_rows[:, q * QUAD : (q + 1) * QUAD, :])
+
+        ident = keep.tile([P, P], F32, name="ident")
+        make_identity(nc, ident[:])
+        ones = keep.tile([P, P], BF16, name="ones")
+        nc.vector.memset(ones[:], 1.0)
+        minus_half = keep.tile([P, 1], F32, name="minus_half")
+        nc.vector.memset(minus_half[:], -0.5)
+        bias_row = keep.tile([P, HID + 2 * OUT], BF16, name="bias_row")
+        nc.vector.memset(bias_row[:], 0.0)
+        gain_rows = keep.tile([P, P], BF16, name="gain_rows")
+        nc.vector.memset(gain_rows[:], 0.0)
+
+        load_h0(0)
+        nc.scalar.dma_start(out=bias_row[0:1, 0:HID], in_=b1.unsqueeze(0))
+        nc.scalar.dma_start(out=bias_row[0:1, HID : HID + OUT], in_=b2.unsqueeze(0))
+        nc.scalar.dma_start(out=gain_rows[0:U_TILES, :], in_=ln1_g.rearrange("(u p) -> u p", p=P))
+        nc.scalar.dma_start(
+            out=gain_rows[U_TILES : 2 * U_TILES, :], in_=ln1_b.rearrange("(u p) -> u p", p=P)
+        )
+
+        def turn_h0(n):
+            words = h0_sb[n // QUAD][:, n % QUAD, :].bitcast(F32)
+            turned = psum.tile([P, PACK, P], F32, name="h0_turned", bufs=1)
+            for s in range(PACK):
+                nc.tensor.transpose(turned[:, s, :], words[:, s * P : (s + 1) * P], ident[:])
+            h0_grouped[n] = feed.tile([P, HID], BF16, name="h0_grouped", bufs=QUAD, align_bytes=64)
+            nc.scalar.copy(
+                out=h0_grouped[n][:].bitcast(F32).rearrange("p (g r u) -> p g r u", g=PASSES, u=2),
+                in_=turned[:].rearrange("p (g u) r -> p g r u", u=2),
+            )
+
+        def pack_h0(n):
+            h0_codes[n] = feed.tile([P, PASSES * P], U32, name="h0_codes", bufs=2 * QUAD, align_bytes=64)
+            h0_scales[n] = feed.tile([P, PASSES * P], U8, name="h0_scales", bufs=2 * QUAD, align_bytes=64)
+            nc.vector.quantize_mx(
+                out=h0_codes[n][:].bitcast(FP8X4), scales=h0_scales[n][:], in_=h0_grouped[n][:]
+            )
+
+        def first_layer(n):
+            pre[n] = work.tile([P, HID], F32, name="pre", bufs=2 * QUAD)
+            for h in range(HALVES):
+                cols = slice(h * BANK, (h + 1) * BANK)
+                acc = psum.tile([P, BANK], F32, name="acc", bufs=4)
+                for g in range(PASSES):
+                    rows = slice(g * P, (g + 1) * P)
+                    nc.tensor.matmul_mx(
+                        out=acc[:],
+                        lhsT=h0_codes[n][:, rows].bitcast(FP8X4),
+                        lhsT_scale=h0_scales[n][:, rows],
+                        rhs=w1_codes[:, g, cols].bitcast(FP8X4),
+                        rhs_scale=w1_scales[:, g, cols],
+                        start=(g == 0),
+                        stop=(g == PASSES - 1),
+                    )
+                nc.vector.tensor_tensor(
+                    out=pre[n][:, cols], in0=acc[:], in1=b1_all[:, cols], op=ALU.add
+                )
+
+        def exponential(n):
+            act[n] = work.tile([P, HID], F32, name="act", bufs=3 * QUAD)
+            nc.scalar.activation(out=act[n][:], in_=pre[n][:], func=FUNC.Exp)
+
+        def softplus(n):
+            nc.scalar.activation(out=act[n][:], in_=act[n][:], func=FUNC.Ln, bias=1.0)
+
+        def tanh(n):
+            nc.scalar.activation(out=act[n][:], in_=act[n][:], func=FUNC.Tanh)
+
+        def mish_and_statistics(n):
+            nc.vector.tensor_tensor(out=act[n][:], in0=pre[n][:], in1=act[n][:], op=ALU.mult)
+            partial = work.tile([P, HALVES, 6], F32, name="partial", bufs=4)
+            for h in range(HALVES):
+                nc.vector.bn_stats(out=partial[:, h, :], in_=act[n][:, h * BANK : (h + 1) * BANK])
+            stats[n] = work.tile([P, 2], F32, name="stats", bufs=4)
+            nc.vector.bn_aggr(out=stats[n][:], in_=partial[:].rearrange("p h s -> p (h s)"))
+            shifted = work.tile([P, 1], F32, name="shifted", bufs=4)
+            nc.gpsimd.tensor_scalar(
+                out=shifted[:], in0=stats[n][:, 1:2], scalar1=LN_EPS, scalar2=1.0,
+                op0=ALU.add, op1=ALU.mult,
+            )
+            rstd[n] = work.tile([P, 1], F32, name="rstd", bufs=4)
+            nc.gpsimd.tensor_tensor(out=rstd[n][:], in0=shifted[:], in1=minus_half[:], op=ALU.pow)
+
+        def normalise(n):
+            nc.vector.tensor_scalar(
+                out=act[n][:], in0=act[n][:], scalar1=stats[n][:, 0:1], scalar2=rstd[n][:],
+                op0=ALU.subtract, op1=ALU.mult,
+            )
+
+        def turn_and_scale(q, u):
+            if u == 0:
+                h1[q] = work.tile([P, U_TILES, QUAD * P], BF16, name="h1", bufs=2)
+            turned = psum.tile([P, QUAD, P], F32, name="act_turned", bufs=2)
+            for j in range(QUAD):
+                nc.tensor.transpose(
+                    turned[:, j, :], act[q * QUAD + j][:, u * P : (u + 1) * P], ident[:]
+                )
+            nc.scalar.activation(
+                out=h1[q][:, u, :],
+                in_=turned[:].rearrange("p j r -> p (j r)"),
+                func=FUNC.Identity,
+                scale=gains[:, u : u + 1],
+                bias=gains[:, U_TILES + u : U_TILES + u + 1],
+            )
+
+        def quantise_h1(q):
+            h1_codes[q] = work.tile([P, PASSES, QUAD * P], U32, name="h1_codes", bufs=2, align_bytes=64)
+            h1_scales[q] = work.tile([P, PASSES, QUAD * P], U8, name="h1_scales", bufs=2, align_bytes=64)
+            for g in range(PASSES):
+                grouped = work.tile([P, QUAD * P, PACK], BF16, name="h1_grouped", bufs=2, align_bytes=64)
+                interleave_four(nc.vector.tensor_copy, grouped[:], h1[q][:, g * PACK : (g + 1) * PACK, :])
+                nc.vector.quantize_mx(
+                    out=h1_codes[q][:, g, :].bitcast(FP8X4),
+                    scales=h1_scales[q][:, g, :],
+                    in_=grouped[:].rearrange("p c t -> p (c t)"),
+                )
+
+        def second_layer(q):
+            head[q] = psum.tile([P, QUAD, OUT], F32, name="head", bufs=1)
+            for j in range(QUAD):
+                rows = slice(j * P, (j + 1) * P)
+                for g in range(PASSES):
+                    nc.tensor.matmul_mx(
+                        out=head[q][:, j, :],
+                        lhsT=h1_codes[q][:, g, rows].bitcast(FP8X4),
+                        lhsT_scale=h1_scales[q][:, g, rows],
+                        rhs=w2_codes[:, g, :].bitcast(FP8X4),
+                        rhs_scale=w2_scales[:, g, :],
+                        start=(g == 0),
+                        stop=(g == PASSES - 1),
+                    )
+
+        def corrector_base(q):
+            tiles = slice(q * QUAD, (q + 1) * QUAD)
+            base[q] = work.tile([P, QUAD, OUT], F32, name="base", bufs=2)
+            nc.vector.scalar_tensor_tensor(
+                out=base[q][:], in0=k1_sb[:, tiles, :], scalar=STEP, in1=z_sb[:, tiles, :],
+                op0=ALU.mult, op1=ALU.add,
+            )
+            nc.vector.tensor_tensor(
+                out=base[q][:], in0=base[q][:],
+                in1=b2_step[:].unsqueeze(1).to_broadcast([P, QUAD, OUT]), op=ALU.add,
+            )
+
+        def corrector(q):
+            result = work.tile([P, QUAD, OUT], F32, name="result", bufs=2)
+            nc.vector.scalar_tensor_tensor(
+                out=result[:], in0=head[q][:], scalar=STEP, in1=base[q][:],
+                op0=ALU.mult, op1=ALU.add,
+            )
+            nc.sync.dma_start(out=out_rows[:, q * QUAD : (q + 1) * QUAD, :], in_=result[:])
+
+        w1_codes = keep.tile([P, PASSES, HID], U32, name="w1_codes", align_bytes=64)
+        w1_scales = keep.tile([P, PASSES, HID], U8, name="w1_scales", align_bytes=64)
+        w2_codes = keep.tile([P, PASSES, OUT], U32, name="w2_codes", align_bytes=64)
+        w2_scales = keep.tile([P, PASSES, OUT], U8, name="w2_scales", align_bytes=64)
+        b1_all = keep.tile([P, HID], F32, name="b1_all")
+        b2_step = keep.tile([P, OUT], F32, name="b2_step")
+        gains = keep.tile([P, 2 * U_TILES], F32, name="gains")
+        z_sb = keep.tile([P, TILES, OUT], BF16, name="z_sb")
+        k1_sb = keep.tile([P, TILES, OUT], BF16, name="k1_sb")
+
+        with tc.tile_pool(name="prep", bufs=1) as prep:
+            w1_raw = prep.tile([P, PASSES, PACK, HID], BF16, name="w1_raw")
+            for g in range(PASSES):
+                for u in range(2):
+                    first = g * K_PASS + u * 2 * P
+                    nc.sync.dma_start(
+                        out=w1_raw[:, g, 2 * u : 2 * u + 2, :],
+                        in_=W1[first : first + 2 * P, :].rearrange("(q e) c -> q e c", e=2),
+                    )
+            w2_raw = prep.tile([P, PASSES * PACK, OUT], BF16, name="w2_raw")
+            nc.scalar.dma_start(out=w2_raw[:], in_=W2.rearrange("(s p) c -> p s c", p=P))
+            load_h0(1)
+            nc.sync.dma_start(out=z_sb[:], in_=z_rows)
+            nc.sync.dma_start(out=k1_sb[:], in_=k1_rows)
+
+            for h in range(HALVES):
+                cols = slice(h * BANK, (h + 1) * BANK)
+                spread = psum.tile([P, BANK], F32, name="acc", bufs=4)
+                nc.tensor.matmul(out=spread[:], lhsT=ones[:], rhs=bias_row[:, cols], start=True, stop=True)
+                nc.scalar.copy(out=b1_all[:, cols], in_=spread[:])
+            spread = psum.tile([P, BANK], F32, name="acc", bufs=4)
+            nc.tensor.matmul(
+                out=spread[:, 0 : 2 * OUT], lhsT=ones[:], rhs=bias_row[:, HID : HID + 2 * OUT],
+                start=True, stop=True,
+            )
+            nc.scalar.mul(out=b2_step[:], in_=spread[:, 0:OUT], mul=STEP)
+            gain_f32 = prep.tile([P, P], F32, name="gain_f32")
+            nc.vector.tensor_copy(out=gain_f32[:], in_=gain_rows[:])
+            spread = psum.tile([P, BANK], F32, name="acc", bufs=4)
+            nc.tensor.transpose(spread[:, 0:P], gain_f32[:], ident[:])
+            nc.vector.tensor_copy(out=gains[:], in_=spread[:, 0 : 2 * U_TILES])
+
+            for n in range(QUAD):
+                turn_h0(n)
+                pack_h0(n)
+
+            w1_grouped = {}
+            for g in range(PASSES):
+                for h in range(HALVES):
+                    w1_grouped[g, h] = prep.tile(
+                        [P, BANK, PACK], BF16, name="w1_grouped", bufs=PASSES * HALVES, align_bytes=64
+                    )
+                    interleave_four(
+                        nc.vector.tensor_copy if h == 0 else nc.scalar.copy,
+                        w1_grouped[g, h][:],
+                        w1_raw[:, g, :, h * BANK : (h + 1) * BANK],
+                    )
+            for h in range(HALVES):
+                for g in range(PASSES):
+                    cols = slice(h * BANK, (h + 1) * BANK)
+                    nc.vector.quantize_mx(
+                        out=w1_codes[:, g, cols].bitcast(FP8X4),
+                        scales=w1_scales[:, g, cols],
+                        in_=w1_grouped[g, h][:].rearrange("p c t -> p (c t)"),
+                    )
+            w2_grouped = prep.tile([P, PASSES, OUT, PACK], BF16, name="w2_grouped", align_bytes=64)
+            for g in range(PASSES):
+                interleave_four(
+                    nc.vector.tensor_copy, w2_grouped[:, g, :, :], w2_raw[:, g * PACK : (g + 1) * PACK, :]
+                )
+            nc.vector.quantize_mx(
+                out=w2_codes[:].rearrange("p g c -> p (g c)").bitcast(FP8X4),
+                scales=w2_scales[:].rearrange("p g c -> p (g c)"),
+                in_=w2_grouped[:].rearrange("p g c t -> p (g c t)"),
+            )
+
+        work = ctx.enter_context(tc.tile_pool(name="work", bufs=1))
+        banks_a_tile = U_TILES // QUAD
+
+        def live(q):
+            return 0 <= q < QUADS
+
+        for i in range(-1, QUADS + 2):
+            if live(i + 3):
+                load_h0(i + 3)
+            for j in range(QUAD):
+                if live(i - 1):
+                    tanh((i - 1) * QUAD + j)
+                if live(i - 2):
+                    for u in range(j * banks_a_tile, (j + 1) * banks_a_tile):
+                        turn_and_scale(i - 2, u)
+                if live(i - 1):
+                    mish_and_statistics((i - 1) * QUAD + j)
+                    if j > 0:
+                        normalise((i - 1) * QUAD + j - 1)
+                if live(i + 1):
+                    first_layer((i + 1) * QUAD + j)
+            if live(i - 1):
+                normalise((i - 1) * QUAD + QUAD - 1)
+            for j in range(QUAD):
+                if live(i):
+                    exponential(i * QUAD + j)
+                if live(i + 2):
+                    turn_h0((i + 2) * QUAD + j)
+            if live(i):
+                for j in range(QUAD):
+                    softplus(i * QUAD + j)
+            if live(i - 2):
+                corrector_base(i - 2)
+                quantise_h1(i - 2)
+                second_layer(i - 2)
+            if live(i + 2):
+                for j in range(QUAD):
+                    pack_h0((i + 2) * QUAD + j)
+            if live(i - 2):
+                corrector(i - 2)

@@ -48,8 +48,8 @@ def tile_actorflowode_pb_t_kernel(tc, h0, z, k1, W1, b1, ln1_g, ln1_b, W2, b2, o
         feed = ctx.enter_context(tc.tile_pool(name="feed", bufs=1))
         psum = ctx.enter_context(tc.psum_pool(name="psum", bufs=1))
 
-        h0_sb, h0_grouped, h0_codes, h0_scales = {}, {}, {}, {}
-        pre, act, stats, rstd = {}, {}, {}, {}
+        h0_sb, h0_turned, h0_grouped, h0_codes, h0_scales = {}, {}, {}, {}, {}
+        sums, pre, act, minus_mean, rstd = {}, {}, {}, {}, {}
         h1, h1_codes, h1_scales, head, base = {}, {}, {}, {}, {}
 
         def load_h0(q):
@@ -77,13 +77,15 @@ def tile_actorflowode_pb_t_kernel(tc, h0, z, k1, W1, b1, ln1_g, ln1_b, W2, b2, o
 
         def turn_h0(n):
             words = h0_sb[n // QUAD][:, n % QUAD, :].bitcast(F32)
-            turned = psum.tile([P, PACK, P], F32, name="h0_turned", bufs=1)
+            h0_turned[n] = psum.tile([P, PACK, P], F32, name="h0_turned", bufs=1)
             for s in range(PACK):
-                nc.tensor.transpose(turned[:, s, :], words[:, s * P : (s + 1) * P], ident[:])
+                nc.tensor.transpose(h0_turned[n][:, s, :], words[:, s * P : (s + 1) * P], ident[:])
+
+        def group_h0(n, copy):
             h0_grouped[n] = feed.tile([P, HID], BF16, name="h0_grouped", bufs=QUAD, align_bytes=64)
-            nc.scalar.copy(
+            copy(
                 out=h0_grouped[n][:].bitcast(F32).rearrange("p (g r u) -> p g r u", g=PASSES, u=2),
-                in_=turned[:].rearrange("p (g u) r -> p g r u", u=2),
+                in_=h0_turned[n][:].rearrange("p (g u) r -> p g r u", u=2),
             )
 
         def pack_h0(n):
@@ -94,10 +96,10 @@ def tile_actorflowode_pb_t_kernel(tc, h0, z, k1, W1, b1, ln1_g, ln1_b, W2, b2, o
             )
 
         def first_layer(n):
-            pre[n] = work.tile([P, HID], F32, name="pre", bufs=2 * QUAD)
             for h in range(HALVES):
                 cols = slice(h * BANK, (h + 1) * BANK)
-                acc = psum.tile([P, BANK], F32, name="acc", bufs=4)
+                acc = psum.tile([P, BANK], F32, name="acc", bufs=2 * HALVES)
+                sums[n, h] = acc
                 for g in range(PASSES):
                     rows = slice(g * P, (g + 1) * P)
                     nc.tensor.matmul_mx(
@@ -109,8 +111,13 @@ def tile_actorflowode_pb_t_kernel(tc, h0, z, k1, W1, b1, ln1_g, ln1_b, W2, b2, o
                         start=(g == 0),
                         stop=(g == PASSES - 1),
                     )
+
+        def add_bias(n):
+            pre[n] = work.tile([P, HID], F32, name="pre", bufs=2 * QUAD)
+            for h in range(HALVES):
+                cols = slice(h * BANK, (h + 1) * BANK)
                 nc.vector.tensor_tensor(
-                    out=pre[n][:, cols], in0=acc[:], in1=b1_all[:, cols], op=ALU.add
+                    out=pre[n][:, cols], in0=sums[n, h][:], in1=b1_all[:, cols], op=ALU.add
                 )
 
         def exponential(n):
@@ -128,20 +135,25 @@ def tile_actorflowode_pb_t_kernel(tc, h0, z, k1, W1, b1, ln1_g, ln1_b, W2, b2, o
             partial = work.tile([P, HALVES, 6], F32, name="partial", bufs=4)
             for h in range(HALVES):
                 nc.vector.bn_stats(out=partial[:, h, :], in_=act[n][:, h * BANK : (h + 1) * BANK])
-            stats[n] = work.tile([P, 2], F32, name="stats", bufs=4)
-            nc.vector.bn_aggr(out=stats[n][:], in_=partial[:].rearrange("p h s -> p (h s)"))
+            stats = work.tile([P, 2], F32, name="stats", bufs=4)
+            nc.vector.bn_aggr(out=stats[:], in_=partial[:].rearrange("p h s -> p (h s)"))
             shifted = work.tile([P, 1], F32, name="shifted", bufs=4)
             nc.gpsimd.tensor_scalar(
-                out=shifted[:], in0=stats[n][:, 1:2], scalar1=LN_EPS, scalar2=1.0,
+                out=shifted[:], in0=stats[:, 1:2], scalar1=LN_EPS, scalar2=1.0,
                 op0=ALU.add, op1=ALU.mult,
             )
             rstd[n] = work.tile([P, 1], F32, name="rstd", bufs=4)
             nc.gpsimd.tensor_tensor(out=rstd[n][:], in0=shifted[:], in1=minus_half[:], op=ALU.pow)
+            minus_mean[n] = work.tile([P, 1], F32, name="minus_mean", bufs=4)
+            nc.gpsimd.tensor_scalar(
+                out=minus_mean[n][:], in0=stats[:, 0:1], scalar1=-1.0, scalar2=0.0,
+                op0=ALU.mult, op1=ALU.add,
+            )
 
         def normalise(n):
-            nc.vector.tensor_scalar(
-                out=act[n][:], in0=act[n][:], scalar1=stats[n][:, 0:1], scalar2=rstd[n][:],
-                op0=ALU.subtract, op1=ALU.mult,
+            nc.gpsimd.tensor_scalar(
+                out=act[n][:], in0=act[n][:], scalar1=minus_mean[n][:], scalar2=rstd[n][:],
+                op0=ALU.add, op1=ALU.mult,
             )
 
         def turn_and_scale(q, u):
@@ -163,13 +175,19 @@ def tile_actorflowode_pb_t_kernel(tc, h0, z, k1, W1, b1, ln1_g, ln1_b, W2, b2, o
         def quantise_h1(q):
             h1_codes[q] = work.tile([P, PASSES, QUAD * P], U32, name="h1_codes", bufs=2, align_bytes=64)
             h1_scales[q] = work.tile([P, PASSES, QUAD * P], U8, name="h1_scales", bufs=2, align_bytes=64)
+            grouped = {}
             for g in range(PASSES):
-                grouped = work.tile([P, QUAD * P, PACK], BF16, name="h1_grouped", bufs=2, align_bytes=64)
-                interleave_four(nc.vector.tensor_copy, grouped[:], h1[q][:, g * PACK : (g + 1) * PACK, :])
+                grouped[g] = work.tile(
+                    [P, QUAD * P, PACK], BF16, name="h1_grouped", bufs=PASSES, align_bytes=64
+                )
+                interleave_four(
+                    nc.vector.tensor_copy, grouped[g][:], h1[q][:, g * PACK : (g + 1) * PACK, :]
+                )
+            for g in range(PASSES):
                 nc.vector.quantize_mx(
                     out=h1_codes[q][:, g, :].bitcast(FP8X4),
                     scales=h1_scales[q][:, g, :],
-                    in_=grouped[:].rearrange("p c t -> p (c t)"),
+                    in_=grouped[g][:].rearrange("p c t -> p (c t)"),
                 )
 
         def second_layer(q):
@@ -190,11 +208,12 @@ def tile_actorflowode_pb_t_kernel(tc, h0, z, k1, W1, b1, ln1_g, ln1_b, W2, b2, o
         def corrector_base(q):
             tiles = slice(q * QUAD, (q + 1) * QUAD)
             base[q] = work.tile([P, QUAD, OUT], F32, name="base", bufs=2)
-            nc.vector.scalar_tensor_tensor(
-                out=base[q][:], in0=k1_sb[:, tiles, :], scalar=STEP, in1=z_sb[:, tiles, :],
+            nc.gpsimd.tensor_scalar(
+                out=base[q][:], in0=k1_sb[:, tiles, :], scalar1=STEP, scalar2=0.0,
                 op0=ALU.mult, op1=ALU.add,
             )
-            nc.vector.tensor_tensor(
+            nc.gpsimd.tensor_tensor(out=base[q][:], in0=base[q][:], in1=z_sb[:, tiles, :], op=ALU.add)
+            nc.gpsimd.tensor_tensor(
                 out=base[q][:], in0=base[q][:],
                 in1=b2_step[:].unsqueeze(1).to_broadcast([P, QUAD, OUT]), op=ALU.add,
             )
@@ -249,12 +268,12 @@ def tile_actorflowode_pb_t_kernel(tc, h0, z, k1, W1, b1, ln1_g, ln1_b, W2, b2, o
             nc.tensor.transpose(spread[:, 0:P], gain_f32[:], ident[:])
             nc.vector.tensor_copy(out=gains[:], in_=spread[:, 0 : 2 * U_TILES])
 
-            for n in range(QUAD):
-                turn_h0(n)
-                pack_h0(n)
-
             w1_grouped = {}
             for g in range(PASSES):
+                pair = range(g * QUAD // PASSES, (g + 1) * QUAD // PASSES)
+                for n in pair:
+                    turn_h0(n)
+                    group_h0(n, nc.scalar.copy)
                 for h in range(HALVES):
                     w1_grouped[g, h] = prep.tile(
                         [P, BANK, PACK], BF16, name="w1_grouped", bufs=PASSES * HALVES, align_bytes=64
@@ -264,6 +283,8 @@ def tile_actorflowode_pb_t_kernel(tc, h0, z, k1, W1, b1, ln1_g, ln1_b, W2, b2, o
                         w1_grouped[g, h][:],
                         w1_raw[:, g, :, h * BANK : (h + 1) * BANK],
                     )
+                for n in pair:
+                    pack_h0(n)
             for h in range(HALVES):
                 for g in range(PASSES):
                     cols = slice(h * BANK, (h + 1) * BANK)
@@ -285,6 +306,7 @@ def tile_actorflowode_pb_t_kernel(tc, h0, z, k1, W1, b1, ln1_g, ln1_b, W2, b2, o
 
         work = ctx.enter_context(tc.tile_pool(name="work", bufs=1))
         banks_a_tile = U_TILES // QUAD
+        ahead = 2
 
         def live(q):
             return 0 <= q < QUADS
@@ -298,28 +320,35 @@ def tile_actorflowode_pb_t_kernel(tc, h0, z, k1, W1, b1, ln1_g, ln1_b, W2, b2, o
                 if live(i - 2):
                     for u in range(j * banks_a_tile, (j + 1) * banks_a_tile):
                         turn_and_scale(i - 2, u)
-                if live(i - 1):
-                    mish_and_statistics((i - 1) * QUAD + j)
-                    if j > 0:
-                        normalise((i - 1) * QUAD + j - 1)
-                if live(i + 1):
-                    first_layer((i + 1) * QUAD + j)
             if live(i - 1):
-                normalise((i - 1) * QUAD + QUAD - 1)
-            for j in range(QUAD):
-                if live(i):
-                    exponential(i * QUAD + j)
-                if live(i + 2):
-                    turn_h0((i + 2) * QUAD + j)
+                for n in range((i - 1) * QUAD, i * QUAD):
+                    mish_and_statistics(n)
+                    normalise(n)
             if live(i):
-                for j in range(QUAD):
-                    softplus(i * QUAD + j)
+                for n in range(i * QUAD, (i + 1) * QUAD):
+                    exponential(n)
+                for n in range(i * QUAD, (i + 1) * QUAD):
+                    softplus(n)
+            if live(i + 1):
+                for j in range(ahead):
+                    first_layer((i + 1) * QUAD + j)
+            if live(i + 2):
+                turn_h0((i + 2) * QUAD)
             if live(i - 2):
                 corrector_base(i - 2)
                 quantise_h1(i - 2)
                 second_layer(i - 2)
+            for j in range(QUAD):
+                if live(i + 1):
+                    add_bias((i + 1) * QUAD + j)
+                    if j + ahead < QUAD:
+                        first_layer((i + 1) * QUAD + j + ahead)
+                if live(i + 2):
+                    group_h0((i + 2) * QUAD + j, nc.vector.tensor_copy)
+                    if j + 1 < QUAD:
+                        turn_h0((i + 2) * QUAD + j + 1)
             if live(i + 2):
-                for j in range(QUAD):
-                    pack_h0((i + 2) * QUAD + j)
+                for n in range((i + 2) * QUAD, (i + 3) * QUAD):
+                    pack_h0(n)
             if live(i - 2):
                 corrector(i - 2)

@@ -50,7 +50,7 @@ def tile_actorflowode_pb_t_kernel(tc, h0, z, k1, W1, b1, ln1_g, ln1_b, W2, b2, o
 
         h0_sb, h0_turned, h0_grouped, h0_codes, h0_scales = {}, {}, {}, {}, {}
         sums, pre, act, minus_mean, rstd = {}, {}, {}, {}, {}
-        h1, h1_codes, h1_scales, head, base = {}, {}, {}, {}, {}
+        h1, h1_codes, h1_scales, head = {}, {}, {}, {}
 
         def load_h0(q):
             h0_sb[q] = feed.tile([P, QUAD, HID], BF16, name="h0_sb", bufs=3)
@@ -205,23 +205,10 @@ def tile_actorflowode_pb_t_kernel(tc, h0, z, k1, W1, b1, ln1_g, ln1_b, W2, b2, o
                         stop=(g == PASSES - 1),
                     )
 
-        def corrector_base(q):
-            tiles = slice(q * QUAD, (q + 1) * QUAD)
-            base[q] = work.tile([P, QUAD, OUT], F32, name="base", bufs=2)
-            nc.gpsimd.tensor_scalar(
-                out=base[q][:], in0=k1_sb[:, tiles, :], scalar1=STEP, scalar2=0.0,
-                op0=ALU.mult, op1=ALU.add,
-            )
-            nc.gpsimd.tensor_tensor(out=base[q][:], in0=base[q][:], in1=z_sb[:, tiles, :], op=ALU.add)
-            nc.gpsimd.tensor_tensor(
-                out=base[q][:], in0=base[q][:],
-                in1=b2_step[:].unsqueeze(1).to_broadcast([P, QUAD, OUT]), op=ALU.add,
-            )
-
         def corrector(q):
             result = work.tile([P, QUAD, OUT], F32, name="result", bufs=2)
             nc.vector.scalar_tensor_tensor(
-                out=result[:], in0=head[q][:], scalar=STEP, in1=base[q][:],
+                out=result[:], in0=head[q][:], scalar=STEP, in1=base[:, q * QUAD : (q + 1) * QUAD, :],
                 op0=ALU.mult, op1=ALU.add,
             )
             nc.sync.dma_start(out=out_rows[:, q * QUAD : (q + 1) * QUAD, :], in_=result[:])
@@ -235,6 +222,7 @@ def tile_actorflowode_pb_t_kernel(tc, h0, z, k1, W1, b1, ln1_g, ln1_b, W2, b2, o
         gains = keep.tile([P, 2 * U_TILES], F32, name="gains")
         z_sb = keep.tile([P, TILES, OUT], BF16, name="z_sb")
         k1_sb = keep.tile([P, TILES, OUT], BF16, name="k1_sb")
+        base = keep.tile([P, TILES, OUT], F32, name="base")
 
         with tc.tile_pool(name="prep", bufs=1) as prep:
             w1_raw = prep.tile([P, PASSES, PACK, HID], BF16, name="w1_raw")
@@ -304,6 +292,15 @@ def tile_actorflowode_pb_t_kernel(tc, h0, z, k1, W1, b1, ln1_g, ln1_b, W2, b2, o
                 in_=w2_grouped[:].rearrange("p g c t -> p (g c t)"),
             )
 
+        nc.gpsimd.tensor_scalar(
+            out=base[:], in0=k1_sb[:], scalar1=STEP, scalar2=0.0, op0=ALU.mult, op1=ALU.add
+        )
+        nc.gpsimd.tensor_tensor(out=base[:], in0=base[:], in1=z_sb[:], op=ALU.add)
+        nc.gpsimd.tensor_tensor(
+            out=base[:], in0=base[:],
+            in1=b2_step[:].unsqueeze(1).to_broadcast([P, TILES, OUT]), op=ALU.add,
+        )
+
         work = ctx.enter_context(tc.tile_pool(name="work", bufs=1))
         banks_a_tile = U_TILES // QUAD
         ahead = 2
@@ -335,7 +332,6 @@ def tile_actorflowode_pb_t_kernel(tc, h0, z, k1, W1, b1, ln1_g, ln1_b, W2, b2, o
             if live(i + 2):
                 turn_h0((i + 2) * QUAD)
             if live(i - 2):
-                corrector_base(i - 2)
                 quantise_h1(i - 2)
                 second_layer(i - 2)
             for j in range(QUAD):

@@ -49,8 +49,8 @@ def tile_actorflowode_pb_t_kernel(tc, h0, z, k1, W1, b1, ln1_g, ln1_b, W2, b2, o
         psum = ctx.enter_context(tc.psum_pool(name="psum", bufs=1))
 
         h0_sb, h0_turned, h0_grouped, h0_codes, h0_scales = {}, {}, {}, {}, {}
-        sums, pre, act, minus_mean, rstd = {}, {}, {}, {}, {}
-        h1, h1_codes, h1_scales, head = {}, {}, {}, {}
+        sums, pre, act, stats, rstd = {}, {}, {}, {}, {}
+        h1, h1_grouped, h1_codes, h1_scales, head, base = {}, {}, {}, {}, {}, {}
 
         def load_h0(q):
             h0_sb[q] = feed.tile([P, QUAD, HID], BF16, name="h0_sb", bufs=3)
@@ -135,25 +135,20 @@ def tile_actorflowode_pb_t_kernel(tc, h0, z, k1, W1, b1, ln1_g, ln1_b, W2, b2, o
             partial = work.tile([P, HALVES, 6], F32, name="partial", bufs=4)
             for h in range(HALVES):
                 nc.vector.bn_stats(out=partial[:, h, :], in_=act[n][:, h * BANK : (h + 1) * BANK])
-            stats = work.tile([P, 2], F32, name="stats", bufs=4)
-            nc.vector.bn_aggr(out=stats[:], in_=partial[:].rearrange("p h s -> p (h s)"))
+            stats[n] = work.tile([P, 2], F32, name="stats", bufs=4)
+            nc.vector.bn_aggr(out=stats[n][:], in_=partial[:].rearrange("p h s -> p (h s)"))
             shifted = work.tile([P, 1], F32, name="shifted", bufs=4)
             nc.gpsimd.tensor_scalar(
-                out=shifted[:], in0=stats[:, 1:2], scalar1=LN_EPS, scalar2=1.0,
+                out=shifted[:], in0=stats[n][:, 1:2], scalar1=LN_EPS, scalar2=1.0,
                 op0=ALU.add, op1=ALU.mult,
             )
             rstd[n] = work.tile([P, 1], F32, name="rstd", bufs=4)
             nc.gpsimd.tensor_tensor(out=rstd[n][:], in0=shifted[:], in1=minus_half[:], op=ALU.pow)
-            minus_mean[n] = work.tile([P, 1], F32, name="minus_mean", bufs=4)
-            nc.gpsimd.tensor_scalar(
-                out=minus_mean[n][:], in0=stats[:, 0:1], scalar1=-1.0, scalar2=0.0,
-                op0=ALU.mult, op1=ALU.add,
-            )
 
         def normalise(n):
-            nc.gpsimd.tensor_scalar(
-                out=act[n][:], in0=act[n][:], scalar1=minus_mean[n][:], scalar2=rstd[n][:],
-                op0=ALU.add, op1=ALU.mult,
+            nc.vector.tensor_scalar(
+                out=act[n][:], in0=act[n][:], scalar1=stats[n][:, 0:1], scalar2=rstd[n][:],
+                op0=ALU.subtract, op1=ALU.mult,
             )
 
         def turn_and_scale(q, u):
@@ -172,22 +167,22 @@ def tile_actorflowode_pb_t_kernel(tc, h0, z, k1, W1, b1, ln1_g, ln1_b, W2, b2, o
                 bias=gains[:, U_TILES + u : U_TILES + u + 1],
             )
 
-        def quantise_h1(q):
+        def group_h1(q, g):
+            h1_grouped[q, g] = work.tile(
+                [P, QUAD * P, PACK], BF16, name="h1_grouped", bufs=PASSES, align_bytes=64
+            )
+            interleave_four(
+                nc.vector.tensor_copy, h1_grouped[q, g][:], h1[q][:, g * PACK : (g + 1) * PACK, :]
+            )
+
+        def pack_h1(q):
             h1_codes[q] = work.tile([P, PASSES, QUAD * P], U32, name="h1_codes", bufs=2, align_bytes=64)
             h1_scales[q] = work.tile([P, PASSES, QUAD * P], U8, name="h1_scales", bufs=2, align_bytes=64)
-            grouped = {}
-            for g in range(PASSES):
-                grouped[g] = work.tile(
-                    [P, QUAD * P, PACK], BF16, name="h1_grouped", bufs=PASSES, align_bytes=64
-                )
-                interleave_four(
-                    nc.vector.tensor_copy, grouped[g][:], h1[q][:, g * PACK : (g + 1) * PACK, :]
-                )
             for g in range(PASSES):
                 nc.vector.quantize_mx(
                     out=h1_codes[q][:, g, :].bitcast(FP8X4),
                     scales=h1_scales[q][:, g, :],
-                    in_=grouped[g][:].rearrange("p c t -> p (c t)"),
+                    in_=h1_grouped[q, g][:].rearrange("p c t -> p (c t)"),
                 )
 
         def second_layer(q):
@@ -205,10 +200,22 @@ def tile_actorflowode_pb_t_kernel(tc, h0, z, k1, W1, b1, ln1_g, ln1_b, W2, b2, o
                         stop=(g == PASSES - 1),
                     )
 
+        def corrector_base(q):
+            tiles = slice(q * QUAD, (q + 1) * QUAD)
+            base[q] = work.tile([P, QUAD, OUT], F32, name="base", bufs=2)
+            nc.vector.scalar_tensor_tensor(
+                out=base[q][:], in0=k1_sb[:, tiles, :], scalar=STEP, in1=z_sb[:, tiles, :],
+                op0=ALU.mult, op1=ALU.add,
+            )
+            nc.vector.tensor_tensor(
+                out=base[q][:], in0=base[q][:],
+                in1=b2_step[:].unsqueeze(1).to_broadcast([P, QUAD, OUT]), op=ALU.add,
+            )
+
         def corrector(q):
             result = work.tile([P, QUAD, OUT], F32, name="result", bufs=2)
             nc.vector.scalar_tensor_tensor(
-                out=result[:], in0=head[q][:], scalar=STEP, in1=base[:, q * QUAD : (q + 1) * QUAD, :],
+                out=result[:], in0=head[q][:], scalar=STEP, in1=base[q][:],
                 op0=ALU.mult, op1=ALU.add,
             )
             nc.sync.dma_start(out=out_rows[:, q * QUAD : (q + 1) * QUAD, :], in_=result[:])
@@ -222,7 +229,6 @@ def tile_actorflowode_pb_t_kernel(tc, h0, z, k1, W1, b1, ln1_g, ln1_b, W2, b2, o
         gains = keep.tile([P, 2 * U_TILES], F32, name="gains")
         z_sb = keep.tile([P, TILES, OUT], BF16, name="z_sb")
         k1_sb = keep.tile([P, TILES, OUT], BF16, name="k1_sb")
-        base = keep.tile([P, TILES, OUT], F32, name="base")
 
         with tc.tile_pool(name="prep", bufs=1) as prep:
             w1_raw = prep.tile([P, PASSES, PACK, HID], BF16, name="w1_raw")
@@ -292,18 +298,10 @@ def tile_actorflowode_pb_t_kernel(tc, h0, z, k1, W1, b1, ln1_g, ln1_b, W2, b2, o
                 in_=w2_grouped[:].rearrange("p g c t -> p (g c t)"),
             )
 
-        nc.gpsimd.tensor_scalar(
-            out=base[:], in0=k1_sb[:], scalar1=STEP, scalar2=0.0, op0=ALU.mult, op1=ALU.add
-        )
-        nc.gpsimd.tensor_tensor(out=base[:], in0=base[:], in1=z_sb[:], op=ALU.add)
-        nc.gpsimd.tensor_tensor(
-            out=base[:], in0=base[:],
-            in1=b2_step[:].unsqueeze(1).to_broadcast([P, TILES, OUT]), op=ALU.add,
-        )
-
         work = ctx.enter_context(tc.tile_pool(name="work", bufs=1))
         banks_a_tile = U_TILES // QUAD
         ahead = 2
+        SCALAR_COPIES = 3
 
         def live(q):
             return 0 <= q < QUADS
@@ -311,16 +309,21 @@ def tile_actorflowode_pb_t_kernel(tc, h0, z, k1, W1, b1, ln1_g, ln1_b, W2, b2, o
         for i in range(-1, QUADS + 2):
             if live(i + 3):
                 load_h0(i + 3)
+            early = SCALAR_COPIES if live(i - 1) else 0
             for j in range(QUAD):
                 if live(i - 1):
                     tanh((i - 1) * QUAD + j)
                 if live(i - 2):
                     for u in range(j * banks_a_tile, (j + 1) * banks_a_tile):
                         turn_and_scale(i - 2, u)
+                if live(i + 2) and j < early:
+                    turn_h0((i + 2) * QUAD + j)
+                    group_h0((i + 2) * QUAD + j, nc.scalar.copy)
             if live(i - 1):
                 for n in range((i - 1) * QUAD, i * QUAD):
                     mish_and_statistics(n)
-                    normalise(n)
+                    if n > (i - 1) * QUAD:
+                        normalise(n - 1)
             if live(i):
                 for n in range(i * QUAD, (i + 1) * QUAD):
                     exponential(n)
@@ -329,17 +332,23 @@ def tile_actorflowode_pb_t_kernel(tc, h0, z, k1, W1, b1, ln1_g, ln1_b, W2, b2, o
             if live(i + 1):
                 for j in range(ahead):
                     first_layer((i + 1) * QUAD + j)
-            if live(i + 2):
-                turn_h0((i + 2) * QUAD)
+            if live(i + 2) and early < QUAD:
+                turn_h0((i + 2) * QUAD + early)
             if live(i - 2):
-                quantise_h1(i - 2)
+                corrector_base(i - 2)
+                group_h1(i - 2, 0)
+            if live(i - 1):
+                normalise(i * QUAD - 1)
+            if live(i - 2):
+                group_h1(i - 2, 1)
+                pack_h1(i - 2)
                 second_layer(i - 2)
             for j in range(QUAD):
                 if live(i + 1):
                     add_bias((i + 1) * QUAD + j)
                     if j + ahead < QUAD:
                         first_layer((i + 1) * QUAD + j + ahead)
-                if live(i + 2):
+                if live(i + 2) and j >= early:
                     group_h0((i + 2) * QUAD + j, nc.vector.tensor_copy)
                     if j + 1 < QUAD:
                         turn_h0((i + 2) * QUAD + j + 1)

@@ -301,7 +301,7 @@ def tile_actorflowode_pb_t_kernel(tc, h0, z, k1, W1, b1, ln1_g, ln1_b, W2, b2, o
         work = ctx.enter_context(tc.tile_pool(name="work", bufs=1))
         banks_a_tile = U_TILES // QUAD
         ahead = 2
-        SCALAR_COPIES = 3
+        SCALAR_COPIES = 2
 
         def live(q):
             return 0 <= q < QUADS

from contextlib import ExitStack

import concourse.mybir as mybir
from concourse.masks import make_identity

F32 = mybir.dt.float32
BF16 = mybir.dt.bfloat16
U32 = mybir.dt.uint32
U8 = mybir.dt.uint8
FP8X4 = mybir.dt.float8_e4m3fn_x4
FUNC = mybir.ActivationFunctionType
ALU = mybir.AluOpType

P = 128
BATCH, HID, OUT = 4096, 1024, 128
TILES = BATCH // P
QUAD = 4
QUADS = TILES // QUAD
PACK = 4
K_PASS = P * PACK
PASSES = HID // K_PASS
BANK = 512
HALVES = HID // BANK
U_TILES = HID // P
LN_EPS = 1e-5
STEP = 0.25

FLOPS = 2 * BATCH * HID * (HID + OUT)


def interleave_four(copy, dst, src):
    copy(
        out=dst.rearrange("p (c i) t -> p c t i", i=4),
        in_=src.rearrange("p t (c i) -> p c t i", i=4),
    )


def tile_actorflowode_pb_t_kernel(tc, h0, z, k1, W1, b1, ln1_g, ln1_b, W2, b2, out):
    nc = tc.nc
    h0_rows = h0.rearrange("(p n) k -> p n k", n=TILES)
    z_rows = z.rearrange("(p n) c -> p n c", n=TILES)
    k1_rows = k1.rearrange("(p n) c -> p n c", n=TILES)
    out_rows = out.rearrange("(p n) c -> p n c", n=TILES)

    with ExitStack() as ctx:
        ctx.enter_context(tc.manual_schedule())
        keep = ctx.enter_context(tc.tile_pool(name="keep", bufs=1))
        feed = ctx.enter_context(tc.tile_pool(name="feed", bufs=1))
        psum = ctx.enter_context(tc.psum_pool(name="psum", bufs=1))

        h0_sb, h0_turned, h0_grouped, h0_codes, h0_scales = {}, {}, {}, {}, {}
        sums, pre, act, stats, rstd = {}, {}, {}, {}, {}
        h1, h1_grouped, h1_codes, h1_scales, head, base = {}, {}, {}, {}, {}, {}

        def load_h0(q):
            h0_sb[q] = feed.tile([P, QUAD, HID], BF16, name="h0_sb", bufs=3)
            nc.sync.dma_start(out=h0_sb[q][:], in_=h0_rows[:, q * QUAD : (q + 1) * QUAD, :])

        ident = keep.tile([P, P], F32, name="ident")
        make_identity(nc, ident[:])
        ones = keep.tile([P, P], BF16, name="ones")
        nc.vector.memset(ones[:], 1.0)
        minus_half = keep.tile([P, 1], F32, name="minus_half")
        nc.vector.memset(minus_half[:], -0.5)
        bias_row = keep.tile([P, HID + 2 * OUT], BF16, name="bias_row")
        nc.vector.memset(bias_row[:], 0.0)
        gain_rows = keep.tile([P, P], BF16, name="gain_rows")
        nc.vector.memset(gain_rows[:], 0.0)

        load_h0(0)
        nc.scalar.dma_start(out=bias_row[0:1, 0:HID], in_=b1.unsqueeze(0))
        nc.scalar.dma_start(out=bias_row[0:1, HID : HID + OUT], in_=b2.unsqueeze(0))
        nc.scalar.dma_start(out=gain_rows[0:U_TILES, :], in_=ln1_g.rearrange("(u p) -> u p", p=P))
        nc.scalar.dma_start(
            out=gain_rows[U_TILES : 2 * U_TILES, :], in_=ln1_b.rearrange("(u p) -> u p", p=P)
        )

        def turn_h0(n):
            words = h0_sb[n // QUAD][:, n % QUAD, :].bitcast(F32)
            h0_turned[n] = psum.tile([P, PACK, P], F32, name="h0_turned", bufs=1)
            for s in range(PACK):
                nc.tensor.transpose(h0_turned[n][:, s, :], words[:, s * P : (s + 1) * P], ident[:])

        def group_h0(n, copy):
            h0_grouped[n] = feed.tile([P, HID], BF16, name="h0_grouped", bufs=QUAD, align_bytes=64)
            copy(
                out=h0_grouped[n][:].bitcast(F32).rearrange("p (g r u) -> p g r u", g=PASSES, u=2),
                in_=h0_turned[n][:].rearrange("p (g u) r -> p g r u", u=2),
            )

        def pack_h0(n):
            h0_codes[n] = feed.tile([P, PASSES * P], U32, name="h0_codes", bufs=2 * QUAD, align_bytes=64)
            h0_scales[n] = feed.tile([P, PASSES * P], U8, name="h0_scales", bufs=2 * QUAD, align_bytes=64)
            nc.vector.quantize_mx(
                out=h0_codes[n][:].bitcast(FP8X4), scales=h0_scales[n][:], in_=h0_grouped[n][:]
            )

        def first_layer(n):
            for h in range(HALVES):
                cols = slice(h * BANK, (h + 1) * BANK)
                acc = psum.tile([P, BANK], F32, name="acc", bufs=2 * HALVES)
                sums[n, h] = acc
                for g in range(PASSES):
                    rows = slice(g * P, (g + 1) * P)
                    nc.tensor.matmul_mx(
                        out=acc[:],
                        lhsT=h0_codes[n][:, rows].bitcast(FP8X4),
                        lhsT_scale=h0_scales[n][:, rows],
                        rhs=w1_codes[:, g, cols].bitcast(FP8X4),
                        rhs_scale=w1_scales[:, g, cols],
                        start=(g == 0),
                        stop=(g == PASSES - 1),
                    )

        def add_bias(n):
            pre[n] = work.tile([P, HID], F32, name="pre", bufs=2 * QUAD)
            for h in range(HALVES):
                cols = slice(h * BANK, (h + 1) * BANK)
                nc.vector.tensor_tensor(
                    out=pre[n][:, cols], in0=sums[n, h][:], in1=b1_all[:, cols], op=ALU.add
                )

        def exponential(n):
            act[n] = work.tile([P, HID], F32, name="act", bufs=3 * QUAD)
            nc.scalar.activation(out=act[n][:], in_=pre[n][:], func=FUNC.Exp)

        def softplus(n):
            nc.scalar.activation(out=act[n][:], in_=act[n][:], func=FUNC.Ln, bias=1.0)

        def tanh(n):
            nc.scalar.activation(out=act[n][:], in_=act[n][:], func=FUNC.Tanh)

        def mish_and_statistics(n):
            nc.vector.tensor_tensor(out=act[n][:], in0=pre[n][:], in1=act[n][:], op=ALU.mult)
            partial = work.tile([P, HALVES, 6], F32, name="partial", bufs=4)
            for h in range(HALVES):
                nc.vector.bn_stats(out=partial[:, h, :], in_=act[n][:, h * BANK : (h + 1) * BANK])
            stats[n] = work.tile([P, 2], F32, name="stats", bufs=4)
            nc.vector.bn_aggr(out=stats[n][:], in_=partial[:].rearrange("p h s -> p (h s)"))
            shifted = work.tile([P, 1], F32, name="shifted", bufs=4)
            nc.gpsimd.tensor_scalar(
                out=shifted[:], in0=stats[n][:, 1:2], scalar1=LN_EPS, scalar2=1.0,
                op0=ALU.add, op1=ALU.mult,
            )
            rstd[n] = work.tile([P, 1], F32, name="rstd", bufs=4)
            nc.gpsimd.tensor_tensor(out=rstd[n][:], in0=shifted[:], in1=minus_half[:], op=ALU.pow)

        def normalise(n):
            nc.vector.tensor_scalar(
                out=act[n][:], in0=act[n][:], scalar1=stats[n][:, 0:1], scalar2=rstd[n][:],
                op0=ALU.subtract, op1=ALU.mult,
            )

        def turn_and_scale(q, u):
            if u == 0:
                h1[q] = work.tile([P, U_TILES, QUAD * P], BF16, name="h1", bufs=2)
            turned = psum.tile([P, QUAD, P], F32, name="act_turned", bufs=2)
            for j in range(QUAD):
                nc.tensor.transpose(
                    turned[:, j, :], act[q * QUAD + j][:, u * P : (u + 1) * P], ident[:]
                )
            nc.scalar.activation(
                out=h1[q][:, u, :],
                in_=turned[:].rearrange("p j r -> p (j r)"),
                func=FUNC.Identity,
                scale=gains[:, u : u + 1],
                bias=gains[:, U_TILES + u : U_TILES + u + 1],
            )

        def group_h1(q, g):
            h1_grouped[q, g] = work.tile(
                [P, QUAD * P, PACK], BF16, name="h1_grouped", bufs=PASSES, align_bytes=64
            )
            interleave_four(
                nc.vector.tensor_copy, h1_grouped[q, g][:], h1[q][:, g * PACK : (g + 1) * PACK, :]
            )

        def pack_h1(q):
            h1_codes[q] = work.tile([P, PASSES, QUAD * P], U32, name="h1_codes", bufs=2, align_bytes=64)
            h1_scales[q] = work.tile([P, PASSES, QUAD * P], U8, name="h1_scales", bufs=2, align_bytes=64)
            for g in range(PASSES):
                nc.vector.quantize_mx(
                    out=h1_codes[q][:, g, :].bitcast(FP8X4),
                    scales=h1_scales[q][:, g, :],
                    in_=h1_grouped[q, g][:].rearrange("p c t -> p (c t)"),
                )

        def second_layer(q):
            head[q] = psum.tile([P, QUAD, OUT], F32, name="head", bufs=1)
            for j in range(QUAD):
                rows = slice(j * P, (j + 1) * P)
                for g in range(PASSES):
                    nc.tensor.matmul_mx(
                        out=head[q][:, j, :],
                        lhsT=h1_codes[q][:, g, rows].bitcast(FP8X4),
                        lhsT_scale=h1_scales[q][:, g, rows],
                        rhs=w2_codes[:, g, :].bitcast(FP8X4),
                        rhs_scale=w2_scales[:, g, :],
                        start=(g == 0),
                        stop=(g == PASSES - 1),
                    )

        def corrector_base(q):
            tiles = slice(q * QUAD, (q + 1) * QUAD)
            base[q] = work.tile([P, QUAD, OUT], F32, name="base", bufs=2)
            nc.vector.scalar_tensor_tensor(
                out=base[q][:], in0=k1_sb[:, tiles, :], scalar=STEP, in1=z_sb[:, tiles, :],
                op0=ALU.mult, op1=ALU.add,
            )
            nc.vector.tensor_tensor(
                out=base[q][:], in0=base[q][:],
                in1=b2_step[:].unsqueeze(1).to_broadcast([P, QUAD, OUT]), op=ALU.add,
            )

        def corrector(q):
            result = work.tile([P, QUAD, OUT], F32, name="result", bufs=2)
            nc.vector.scalar_tensor_tensor(
                out=result[:], in0=head[q][:], scalar=STEP, in1=base[q][:],
                op0=ALU.mult, op1=ALU.add,
            )
            nc.sync.dma_start(out=out_rows[:, q * QUAD : (q + 1) * QUAD, :], in_=result[:])

        w1_codes = keep.tile([P, PASSES, HID], U32, name="w1_codes", align_bytes=64)
        w1_scales = keep.tile([P, PASSES, HID], U8, name="w1_scales", align_bytes=64)
        w2_codes = keep.tile([P, PASSES, OUT], U32, name="w2_codes", align_bytes=64)
        w2_scales = keep.tile([P, PASSES, OUT], U8, name="w2_scales", align_bytes=64)
        b1_all = keep.tile([P, HID], F32, name="b1_all")
        b2_step = keep.tile([P, OUT], F32, name="b2_step")
        gains = keep.tile([P, 2 * U_TILES], F32, name="gains")
        z_sb = keep.tile([P, TILES, OUT], BF16, name="z_sb")
        k1_sb = keep.tile([P, TILES, OUT], BF16, name="k1_sb")

        with tc.tile_pool(name="prep", bufs=1) as prep:
            w1_raw = prep.tile([P, PASSES, PACK, HID], BF16, name="w1_raw")
            for g in range(PASSES):
                for u in range(2):
                    first = g * K_PASS + u * 2 * P
                    nc.sync.dma_start(
                        out=w1_raw[:, g, 2 * u : 2 * u + 2, :],
                        in_=W1[first : first + 2 * P, :].rearrange("(q e) c -> q e c", e=2),
                    )
            w2_raw = prep.tile([P, PASSES * PACK, OUT], BF16, name="w2_raw")
            nc.scalar.dma_start(out=w2_raw[:], in_=W2.rearrange("(s p) c -> p s c", p=P))
            load_h0(1)
            nc.sync.dma_start(out=z_sb[:], in_=z_rows)
            nc.sync.dma_start(out=k1_sb[:], in_=k1_rows)

            for h in range(HALVES):
                cols = slice(h * BANK, (h + 1) * BANK)
                spread = psum.tile([P, BANK], F32, name="acc", bufs=4)
                nc.tensor.matmul(out=spread[:], lhsT=ones[:], rhs=bias_row[:, cols], start=True, stop=True)
                nc.scalar.copy(out=b1_all[:, cols], in_=spread[:])
            spread = psum.tile([P, BANK], F32, name="acc", bufs=4)
            nc.tensor.matmul(
                out=spread[:, 0 : 2 * OUT], lhsT=ones[:], rhs=bias_row[:, HID : HID + 2 * OUT],
                start=True, stop=True,
            )
            nc.scalar.mul(out=b2_step[:], in_=spread[:, 0:OUT], mul=STEP)
            gain_f32 = prep.tile([P, P], F32, name="gain_f32")
            nc.vector.tensor_copy(out=gain_f32[:], in_=gain_rows[:])
            spread = psum.tile([P, BANK], F32, name="acc", bufs=4)
            nc.tensor.transpose(spread[:, 0:P], gain_f32[:], ident[:])
            nc.vector.tensor_copy(out=gains[:], in_=spread[:, 0 : 2 * U_TILES])

            w1_grouped = {}
            for g in range(PASSES):
                pair = range(g * QUAD // PASSES, (g + 1) * QUAD // PASSES)
                for n in pair:
                    turn_h0(n)
                    group_h0(n, nc.scalar.copy)
                for h in range(HALVES):
                    w1_grouped[g, h] = prep.tile(
                        [P, BANK, PACK], BF16, name="w1_grouped", bufs=PASSES * HALVES, align_bytes=64
                    )
                    interleave_four(
                        nc.vector.tensor_copy if h == 0 else nc.scalar.copy,
                        w1_grouped[g, h][:],
                        w1_raw[:, g, :, h * BANK : (h + 1) * BANK],
                    )
                for n in pair:
                    pack_h0(n)
            for h in range(HALVES):
                for g in range(PASSES):
                    cols = slice(h * BANK, (h + 1) * BANK)
                    nc.vector.quantize_mx(
                        out=w1_codes[:, g, cols].bitcast(FP8X4),
                        scales=w1_scales[:, g, cols],
                        in_=w1_grouped[g, h][:].rearrange("p c t -> p (c t)"),
                    )
            w2_grouped = prep.tile([P, PASSES, OUT, PACK], BF16, name="w2_grouped", align_bytes=64)
            for g in range(PASSES):
                interleave_four(
                    nc.vector.tensor_copy, w2_grouped[:, g, :, :], w2_raw[:, g * PACK : (g + 1) * PACK, :]
                )
            nc.vector.quantize_mx(
                out=w2_codes[:].rearrange("p g c -> p (g c)").bitcast(FP8X4),
                scales=w2_scales[:].rearrange("p g c -> p (g c)"),
                in_=w2_grouped[:].rearrange("p g c t -> p (g c t)"),
            )

        work = ctx.enter_context(tc.tile_pool(name="work", bufs=1))
        banks_a_tile = U_TILES // QUAD
        ahead = 2
        SCALAR_COPIES = 2

        def live(q):
            return 0 <= q < QUADS

        for i in range(-1, QUADS + 2):
            if live(i + 3):
                load_h0(i + 3)
            early = SCALAR_COPIES if live(i - 1) else 0
            for j in range(QUAD):
                if live(i - 1):
                    tanh((i - 1) * QUAD + j)
                if live(i - 2):
                    for u in range(j * banks_a_tile, (j + 1) * banks_a_tile):
                        turn_and_scale(i - 2, u)
                if live(i + 2) and j < early:
                    turn_h0((i + 2) * QUAD + j)
                    group_h0((i + 2) * QUAD + j, nc.scalar.copy)
            if live(i - 1):
                for n in range((i - 1) * QUAD, i * QUAD):
                    mish_and_statistics(n)
                    if n > (i - 1) * QUAD:
                        normalise(n - 1)
            if live(i):
                for n in range(i * QUAD, (i + 1) * QUAD):
                    exponential(n)
                for n in range(i * QUAD, (i + 1) * QUAD):
                    softplus(n)
            if live(i + 1):
                for j in range(ahead):
                    first_layer((i + 1) * QUAD + j)
            if live(i + 2) and early < QUAD:
                turn_h0((i + 2) * QUAD + early)
            if live(i - 2):
                corrector_base(i - 2)
                group_h1(i - 2, 0)
            if live(i - 1):
                normalise(i * QUAD - 1)
            if live(i - 2):
                group_h1(i - 2, 1)
                pack_h1(i - 2)
                second_layer(i - 2)
            for j in range(QUAD):
                if live(i + 1):
                    add_bias((i + 1) * QUAD + j)
                    if j + ahead < QUAD:
                        first_layer((i + 1) * QUAD + j + ahead)
                if live(i + 2) and j >= early:
                    group_h0((i + 2) * QUAD + j, nc.vector.tensor_copy)
                    if j + 1 < QUAD:
                        turn_h0((i + 2) * QUAD + j + 1)
            if live(i + 2):
                for n in range((i + 2) * QUAD, (i + 3) * QUAD):
                    pack_h0(n)
            if live(i - 2):
                corrector(i - 2)
